import numpy as np
import ml_dtypes


def mxq(x, axis, fmt="e4m3"):
    dtype, down = {"e4m3": (ml_dtypes.float8_e4m3fn, 7), "e5m2": (ml_dtypes.float8_e5m2, 14)}[fmt]
    v = np.moveaxis(np.asarray(x, np.float32).astype(ml_dtypes.bfloat16).astype(np.float64), axis, -1)
    blocks = v.reshape(v.shape[:-1] + (-1, 32))
    amax = np.abs(blocks).max(-1, keepdims=True)
    byte = np.maximum(np.where(amax > 0, np.frexp(amax)[1] - 1 + 127, 0) - down, 1)
    scale = np.exp2(byte - 127.0)
    codes = (blocks / scale).astype(np.float32).astype(dtype).astype(np.float64)
    return np.moveaxis((codes * scale).reshape(v.shape), -1, axis)


WIDE = False


def mx_kscale(k):
    if not WIDE:
        return np.ones(k)
    levels = np.array([10, -10, 5, -5, 0])
    a = np.random.permutation(np.resize(levels, k // 512 * 4)).reshape(k // 512, 4)
    idx = np.arange(k)
    return np.exp2(a[idx // 512, idx % 128 // 32])


BF16 = ml_dtypes.bfloat16


def bf(x):
    return np.asarray(x, np.float32).astype(BF16)


def f64(x):
    return np.asarray(x).astype(np.float64)


B, S, H, I, G = 2, 256, 1024, 2048, 4
T = B * S


def grouped_linear(xf, w, b):
    g, dout, din = w.shape
    xg = xf.reshape(g, -1, din)
    y = (mxq(xg, 2, "e4m3") @ mxq(w, 2, "e4m3").transpose(0, 2, 1)) + b[:, None, :]
    return y.reshape(-1, dout)


def setup_inputs():
    s, t = mx_kscale(H), mx_kscale(I)
    return {"hf": bf(np.random.standard_normal((T, H)) * s),
            "g1_w": bf(np.random.standard_normal((G, I, H)) / np.sqrt(H) / s[None, None, :] * t[None, :, None]),
            "g1_b": bf(np.random.standard_normal((G, I)) * 0.3 * t[None, :]),
            "g2_w": bf(np.random.standard_normal((G, H, I)) / np.sqrt(I) / t[None, None, :]),
            "g2_b": bf(np.random.standard_normal((G, H)) * 0.3)}


def reference(hf, g1_w, g1_b, g2_w, g2_b):
    y = grouped_linear(f64(hf), f64(g1_w), f64(g1_b))
    return grouped_linear(y, f64(g2_w), f64(g2_b))

@@ -1,0 +1,239 @@
+from contextlib import ExitStack
+
+import concourse.mybir as mybir
+from concourse.masks import make_identity
+
+BF16 = mybir.dt.bfloat16
+F32 = mybir.dt.float32
+I32 = mybir.dt.int32
+U32 = mybir.dt.uint32
+U8 = mybir.dt.uint8
+FP8X4 = mybir.dt.float8_e4m3fn_x4
+ADD = mybir.AluOpType.add
+
+P = 128
+GROUPS = 4
+H = 1024
+I = 2048
+K_PASS = 512
+WORDS_PASS = K_PASS // 2
+H_PASSES = H // K_PASS
+I_PASSES = I // K_PASS
+
+CHUNK_TILES = 8
+CHUNKS_PER_GROUP = 4
+CHUNKS_PER_LAYER = GROUPS * CHUNKS_PER_GROUP
+N_CHUNKS = 2 * CHUNKS_PER_LAYER
+W1_ROWS = I // CHUNKS_PER_GROUP
+W2_ROWS = H // CHUNKS_PER_GROUP
+
+RAW_BUFS = 8
+VECTOR_EVERY = 8
+
+FLOPS = 2 * GROUPS * P * H * I * 2
+
+
+def tile_dummytemodel_pa_kernel(tc, hf, g1_w, g1_b, g2_w, g2_b, out):
+    nc = tc.nc
+    with ExitStack() as stack:
+        keep = stack.enter_context(tc.tile_pool(name="keep", bufs=1))
+        raws = stack.enter_context(tc.tile_pool(name="raws", bufs=RAW_BUFS))
+        work = stack.enter_context(tc.tile_pool(name="work", bufs=3))
+        banks = stack.enter_context(tc.psum_pool(name="banks", bufs=6))
+        sums = stack.enter_context(tc.psum_pool(name="sums", bufs=2))
+        stack.enter_context(tc.manual_schedule())
+
+        ident = keep.tile([P, P], F32, name="ident")
+        make_identity(nc, ident[:])
+        ident_bf = keep.tile([P, P], BF16, name="ident_bf")
+        make_identity(nc, ident_bf[:])
+
+        raw = {}
+        x_raw = {}
+        grouped = {}
+        x_grouped = {}
+        codes = {}
+        scales = {}
+        y_grouped = {}
+        out_sb = {}
+        x_codes = [keep.tile([P, H_PASSES, P], U32, name="x_codes%d" % g, align_bytes=64) for g in range(GROUPS)]
+        x_scales = [keep.tile([P, H_PASSES, P], U8, name="x_scales%d" % g, align_bytes=64) for g in range(GROUPS)]
+        y_codes = [keep.tile([P, I_PASSES, P], U32, name="y_codes%d" % g, align_bytes=64) for g in range(GROUPS)]
+        y_scales = [keep.tile([P, I_PASSES, P], U8, name="y_scales%d" % g, align_bytes=64) for g in range(GROUPS)]
+
+        def where(n):
+            layer, rest = divmod(n, CHUNKS_PER_LAYER)
+            g, part = divmod(rest, CHUNKS_PER_GROUP)
+            return layer, g, part
+
+        def load(n):
+            if not 0 <= n < N_CHUNKS:
+                return
+            layer, g, part = where(n)
+            if layer == 0:
+                if part == 0:
+                    x_raw[g] = raws.tile([P, 1, H], BF16, name="x_raw", tag="x_raw", bufs=2)
+                    nc.sync.dma_start(out=x_raw[g][:, 0, :], in_=hf[g * P : (g + 1) * P, :])
+                raw[n] = raws.tile([P, 4, H], BF16, name="raw_w1", tag="raw")
+                rows = g1_w[g, part * W1_ROWS : (part + 1) * W1_ROWS, :]
+                nc.sync.dma_start(
+                    out=raw[n][:].rearrange("p (u e) h -> p u (e h)", u=2),
+                    in_=rows.rearrange("(u p e) h -> p u (e h)", u=2, e=2),
+                )
+            else:
+                raw[n] = raws.tile([P, 2, I], BF16, name="raw_w2", tag="raw")
+                rows = g2_w[g, part * W2_ROWS : (part + 1) * W2_ROWS, :]
+                nc.sync.dma_start(out=raw[n][:], in_=rows.rearrange("(r p) i -> p r i", r=2))
+
+        def flip(raw_tile, operand_tiles, grouped_tile, vector_banks):
+            raw_words = raw_tile[:].bitcast(F32)
+            grouped_words = grouped_tile[:].bitcast(F32)
+            for b in range(len(operand_tiles) // 2):
+                bank = banks.tile([P, 2, 2, P], F32, name="bank", tag="bank")
+                for x in range(2):
+                    row_tile, k_pass = operand_tiles[2 * b + x]
+                    for u in range(2):
+                        first = WORDS_PASS * k_pass + P * u
+                        nc.tensor.transpose(bank[:, x, u, :], raw_words[:, row_tile, first : first + P], ident[:])
+                dst = grouped_words[:, 2 * b : 2 * b + 2, :, :]
+                src = bank[:].rearrange("p x u m -> p x m u")
+                if b in vector_banks:
+                    nc.vector.tensor_copy(out=dst, in_=src)
+                else:
+                    nc.scalar.copy(out=dst, in_=src)
+
+        def spread_b2(g):
+            for half in range(2):
+                b2_bank = banks.tile([P, 512], F32, name="b2_bank", tag="bank")
+                nc.tensor.matmul(
+                    out=b2_bank[:],
+                    lhsT=ident_bf[:, g : g + 1].to_broadcast([P, P]),
+                    rhs=b2_rows[:, half * 512 : (half + 1) * 512],
+                    start=True,
+                    stop=True,
+                )
+                dst = b2[g][:, half * 512 : (half + 1) * 512]
+                if half == 0:
+                    nc.scalar.copy(out=dst, in_=b2_bank[:])
+                else:
+                    nc.vector.tensor_copy(out=dst, in_=b2_bank[:])
+
+        def flip_chunk(n):
+            if not 0 <= n < N_CHUNKS:
+                return
+            layer, g, part = where(n)
+            if layer == 0 and part == 0:
+                x_grouped[g] = work.tile([P, H_PASSES, P, 4], BF16, name="x_grouped", align_bytes=64)
+                flip(x_raw[g], [(0, a) for a in range(H_PASSES)], x_grouped[g], [])
+                spread_b2(g)
+            grouped[n] = work.tile([P, CHUNK_TILES, P, 4], BF16, name="grouped", align_bytes=64)
+            if layer == 0:
+                operand_tiles = [(t, a) for t in range(4) for a in range(H_PASSES)]
+            else:
+                operand_tiles = [(r, c) for c in range(I_PASSES) for r in range(2)]
+            vector_banks = [b for b in range(4) if (4 * n + b) % VECTOR_EVERY == VECTOR_EVERY - 1]
+            flip(raw[n], operand_tiles, grouped[n], vector_banks)
+
+        def quantise(n):
+            if not 0 <= n < N_CHUNKS:
+                return
+            layer, g, part = where(n)
+            if layer == 0 and part == 0:
+                nc.vector.quantize_mx(
+                    out=x_codes[g][:].rearrange("p a k -> p (a k)").bitcast(FP8X4),
+                    scales=x_scales[g][:].rearrange("p a k -> p (a k)"),
+                    in_=x_grouped[g][:].rearrange("p a k t -> p (a k t)"),
+                )
+            codes[n] = work.tile([P, CHUNK_TILES * P], U32, name="codes", align_bytes=64)
+            scales[n] = work.tile([P, CHUNK_TILES * P], U8, name="scales", align_bytes=64)
+            nc.vector.quantize_mx(
+                out=codes[n][:].bitcast(FP8X4),
+                scales=scales[n][:],
+                in_=grouped[n][:].rearrange("p o m t -> p (o m t)"),
+            )
+
+        def multiply(n):
+            if not 0 <= n < N_CHUNKS:
+                return
+            layer, g, part = where(n)
+            if layer == 0:
+                y_bank = sums.tile([P, 4, P], F32, name="y_bank", tag="sum")
+                for t in range(4):
+                    for a in range(H_PASSES):
+                        cols = slice((H_PASSES * t + a) * P, (H_PASSES * t + a + 1) * P)
+                        nc.tensor.matmul_mx(
+                            out=y_bank[:, t, :],
+                            lhsT=codes[n][:, cols].bitcast(FP8X4),
+                            lhsT_scale=scales[n][:, cols],
+                            rhs=x_codes[g][:, a, :].bitcast(FP8X4),
+                            rhs_scale=x_scales[g][:, a, :],
+                            start=(a == 0),
+                            stop=(a == H_PASSES - 1),
+                        )
+                y_grouped[n] = work.tile([P, P, 4], BF16, name="y_grouped", align_bytes=64)
+                first = 4 * (CHUNKS_PER_GROUP * g + part)
+                nc.vector.tensor_tensor(
+                    out=y_grouped[n][:],
+                    in0=y_bank[:].rearrange("p t k -> p k t"),
+                    in1=b1[:, first : first + 4].unsqueeze(1).to_broadcast([P, P, 4]),
+                    op=ADD,
+                )
+            else:
+                out_bank = sums.tile([P, W2_ROWS], F32, name="out_bank", tag="sum")
+                for c in range(I_PASSES):
+                    cols = slice(c * W2_ROWS, (c + 1) * W2_ROWS)
+                    nc.tensor.matmul_mx(
+                        out=out_bank[:],
+                        lhsT=y_codes[g][:, c, :].bitcast(FP8X4),
+                        lhsT_scale=y_scales[g][:, c, :],
+                        rhs=codes[n][:, cols].bitcast(FP8X4),
+                        rhs_scale=scales[n][:, cols],
+                        start=(c == 0),
+                        stop=(c == I_PASSES - 1),
+                    )
+                out_sb[n] = work.tile([P, W2_ROWS], F32, name="out_sb")
+                first = part * W2_ROWS
+                nc.vector.tensor_tensor(
+                    out=out_sb[n][:], in0=out_bank[:], in1=b2[g][:, first : first + W2_ROWS], op=ADD
+                )
+
+        def finish(n):
+            if not 0 <= n < N_CHUNKS:
+                return
+            layer, g, part = where(n)
+            if layer == 0:
+                nc.vector.quantize_mx(
+                    out=y_codes[g][:, part, :].bitcast(FP8X4),
+                    scales=y_scales[g][:, part, :],
+                    in_=y_grouped[n][:].rearrange("p k t -> p (k t)"),
+                )
+            else:
+                nc.sync.dma_start(
+                    out=out[g * P : (g + 1) * P, part * W2_ROWS : (part + 1) * W2_ROWS], in_=out_sb[n][:]
+                )
+
+        b1_rows = keep.tile([P, 2 * P], BF16, name="b1_rows")
+        nc.vector.memset(b1_rows[:].bitcast(I32), 0)
+        b2_rows = keep.tile([P, H], BF16, name="b2_rows")
+        nc.vector.memset(b2_rows[:].bitcast(I32), 0)
+        n_b1_rows = GROUPS * I // (2 * P)
+        nc.sync.dma_start(out=b1_rows[0:n_b1_rows, :], in_=g1_b.rearrange("g (r q) -> (g r) q", q=2 * P))
+        nc.sync.dma_start(out=b2_rows[0:GROUPS, :], in_=g2_b)
+        b2 = [keep.tile([P, H], F32, name="b2_%d" % g) for g in range(GROUPS)]
+
+        for n in range(RAW_BUFS - 1):
+            load(n)
+
+        b1_bank = banks.tile([P, P], F32, name="b1_bank", tag="bank")
+        nc.tensor.transpose(b1_bank[:], b1_rows[:].bitcast(F32), ident[:])
+        b1_pairs = keep.tile([P, 2 * n_b1_rows], BF16, name="b1_pairs")
+        nc.vector.tensor_copy(out=b1_pairs[:].bitcast(F32), in_=b1_bank[:, 0:n_b1_rows])
+        b1 = keep.tile([P, 2 * n_b1_rows], F32, name="b1")
+        nc.vector.tensor_copy(out=b1[:], in_=b1_pairs[:])
+
+        for n in range(N_CHUNKS + 3):
+            finish(n - 3)
+            quantise(n - 1)
+            load(n + RAW_BUFS - 1)
+            flip_chunk(n)
+            multiply(n - 2)

@@ -19,15 +19,14 @@ K_PASS = 512
 WORDS_PASS = K_PASS // 2
 H_PASSES = H // K_PASS
 I_PASSES = I // K_PASS
+BANK = 512
 
+PARTS = 4
+W1_ROWS = I // PARTS
+W2_ROWS = H // PARTS
 CHUNK_TILES = 8
-CHUNKS_PER_GROUP = 4
-CHUNKS_PER_LAYER = GROUPS * CHUNKS_PER_GROUP
-N_CHUNKS = 2 * CHUNKS_PER_LAYER
-W1_ROWS = I // CHUNKS_PER_GROUP
-W2_ROWS = H // CHUNKS_PER_GROUP
 
-RAW_BUFS = 8
+RAW_BUFS = 12
 VECTOR_EVERY = 8
 
 FLOPS = 2 * GROUPS * P * H * I * 2
@@ -35,10 +34,23 @@ FLOPS = 2 * GROUPS * P * H * I * 2
 
 def tile_dummytemodel_pa_kernel(tc, hf, g1_w, g1_b, g2_w, g2_b, out):
     nc = tc.nc
+
+    chunks = []
+    for g in range(GROUPS + 1):
+        for part in range(PARTS):
+            if g < GROUPS:
+                chunks.append((1, g, part * W1_ROWS, W1_ROWS // P))
+            if g > 0:
+                pieces = 2 if (g == GROUPS and part == PARTS - 1) else 1
+                for piece in range(pieces):
+                    rows = W2_ROWS // pieces
+                    chunks.append((2, g - 1, part * W2_ROWS + piece * rows, rows // P))
+    n_chunks = len(chunks)
+
     with ExitStack() as stack:
         keep = stack.enter_context(tc.tile_pool(name="keep", bufs=1))
         raws = stack.enter_context(tc.tile_pool(name="raws", bufs=RAW_BUFS))
-        work = stack.enter_context(tc.tile_pool(name="work", bufs=3))
+        work = stack.enter_context(tc.tile_pool(name="work", bufs=4))
         banks = stack.enter_context(tc.psum_pool(name="banks", bufs=6))
         sums = stack.enter_context(tc.psum_pool(name="sums", bufs=2))
         stack.enter_context(tc.manual_schedule())
@@ -56,36 +68,33 @@ def tile_dummytemodel_pa_kernel(tc, hf, g1_w, g1_b, g2_w, g2_b, out):
         scales = {}
         y_grouped = {}
         out_sb = {}
+        emptied = []
         x_codes = [keep.tile([P, H_PASSES, P], U32, name="x_codes%d" % g, align_bytes=64) for g in range(GROUPS)]
         x_scales = [keep.tile([P, H_PASSES, P], U8, name="x_scales%d" % g, align_bytes=64) for g in range(GROUPS)]
         y_codes = [keep.tile([P, I_PASSES, P], U32, name="y_codes%d" % g, align_bytes=64) for g in range(GROUPS)]
         y_scales = [keep.tile([P, I_PASSES, P], U8, name="y_scales%d" % g, align_bytes=64) for g in range(GROUPS)]
-
-        def where(n):
-            layer, rest = divmod(n, CHUNKS_PER_LAYER)
-            g, part = divmod(rest, CHUNKS_PER_GROUP)
-            return layer, g, part
+        b2 = [keep.tile([P, H], BF16, name="b2_%d" % g) for g in range(GROUPS)]
 
         def load(n):
-            if not 0 <= n < N_CHUNKS:
+            if not 0 <= n < n_chunks:
                 return
-            layer, g, part = where(n)
-            if layer == 0:
-                if part == 0:
+            layer, g, first_row, row_tiles = chunks[n]
+            if layer == 1:
+                if first_row == 0:
                     x_raw[g] = raws.tile([P, 1, H], BF16, name="x_raw", tag="x_raw", bufs=2)
                     nc.sync.dma_start(out=x_raw[g][:, 0, :], in_=hf[g * P : (g + 1) * P, :])
-                raw[n] = raws.tile([P, 4, H], BF16, name="raw_w1", tag="raw")
-                rows = g1_w[g, part * W1_ROWS : (part + 1) * W1_ROWS, :]
+                raw[n] = raws.tile([P, row_tiles, H], BF16, name="raw_w1", tag="raw")
+                rows = g1_w[g, first_row : first_row + W1_ROWS, :]
                 nc.sync.dma_start(
                     out=raw[n][:].rearrange("p (u e) h -> p u (e h)", u=2),
                     in_=rows.rearrange("(u p e) h -> p u (e h)", u=2, e=2),
                 )
             else:
-                raw[n] = raws.tile([P, 2, I], BF16, name="raw_w2", tag="raw")
-                rows = g2_w[g, part * W2_ROWS : (part + 1) * W2_ROWS, :]
-                nc.sync.dma_start(out=raw[n][:], in_=rows.rearrange("(r p) i -> p r i", r=2))
+                raw[n] = raws.tile([P, row_tiles, I], BF16, name="raw_w2", tag="raw")
+                rows = g2_w[g, first_row : first_row + row_tiles * P, :]
+                nc.sync.dma_start(out=raw[n][:], in_=rows.rearrange("(r p) i -> p r i", p=P))
 
-        def flip(raw_tile, operand_tiles, grouped_tile, vector_banks):
+        def flip(raw_tile, operand_tiles, grouped_tile):
             raw_words = raw_tile[:].bitcast(F32)
             grouped_words = grouped_tile[:].bitcast(F32)
             for b in range(len(operand_tiles) // 2):
@@ -97,68 +106,66 @@ def tile_dummytemodel_pa_kernel(tc, hf, g1_w, g1_b, g2_w, g2_b, out):
                         nc.tensor.transpose(bank[:, x, u, :], raw_words[:, row_tile, first : first + P], ident[:])
                 dst = grouped_words[:, 2 * b : 2 * b + 2, :, :]
                 src = bank[:].rearrange("p x u m -> p x m u")
-                if b in vector_banks:
+                if len(emptied) % VECTOR_EVERY == VECTOR_EVERY - 1:
                     nc.vector.tensor_copy(out=dst, in_=src)
                 else:
                     nc.scalar.copy(out=dst, in_=src)
+                emptied.append(b)
 
         def spread_b2(g):
-            for half in range(2):
-                b2_bank = banks.tile([P, 512], F32, name="b2_bank", tag="bank")
+            b2_bank = banks.tile([P, H], BF16, name="b2_bank", tag="bank")
+            for half in range(H // BANK):
+                cols = slice(half * BANK, (half + 1) * BANK)
                 nc.tensor.matmul(
-                    out=b2_bank[:],
+                    out=b2_bank[:, cols],
                     lhsT=ident_bf[:, g : g + 1].to_broadcast([P, P]),
-                    rhs=b2_rows[:, half * 512 : (half + 1) * 512],
+                    rhs=b2_rows[:, cols],
                     start=True,
                     stop=True,
                 )
-                dst = b2[g][:, half * 512 : (half + 1) * 512]
-                if half == 0:
-                    nc.scalar.copy(out=dst, in_=b2_bank[:])
-                else:
-                    nc.vector.tensor_copy(out=dst, in_=b2_bank[:])
+            nc.scalar.copy(out=b2[g][:], in_=b2_bank[:])
 
         def flip_chunk(n):
-            if not 0 <= n < N_CHUNKS:
+            if not 0 <= n < n_chunks:
                 return
-            layer, g, part = where(n)
-            if layer == 0 and part == 0:
+            layer, g, first_row, row_tiles = chunks[n]
+            if layer == 1 and first_row == 0:
                 x_grouped[g] = work.tile([P, H_PASSES, P, 4], BF16, name="x_grouped", align_bytes=64)
-                flip(x_raw[g], [(0, a) for a in range(H_PASSES)], x_grouped[g], [])
+                flip(x_raw[g], [(0, a) for a in range(H_PASSES)], x_grouped[g])
                 spread_b2(g)
             grouped[n] = work.tile([P, CHUNK_TILES, P, 4], BF16, name="grouped", align_bytes=64)
-            if layer == 0:
-                operand_tiles = [(t, a) for t in range(4) for a in range(H_PASSES)]
+            if layer == 1:
+                operand_tiles = [(t, a) for t in range(row_tiles) for a in range(H_PASSES)]
             else:
-                operand_tiles = [(r, c) for c in range(I_PASSES) for r in range(2)]
-            vector_banks = [b for b in range(4) if (4 * n + b) % VECTOR_EVERY == VECTOR_EVERY - 1]
-            flip(raw[n], operand_tiles, grouped[n], vector_banks)
+                operand_tiles = [(r, c) for c in range(I_PASSES) for r in range(row_tiles)]
+            flip(raw[n], operand_tiles, grouped[n])
 
         def quantise(n):
-            if not 0 <= n < N_CHUNKS:
+            if not 0 <= n < n_chunks:
                 return
-            layer, g, part = where(n)
-            if layer == 0 and part == 0:
+            layer, g, first_row, row_tiles = chunks[n]
+            if layer == 1 and first_row == 0:
                 nc.vector.quantize_mx(
                     out=x_codes[g][:].rearrange("p a k -> p (a k)").bitcast(FP8X4),
                     scales=x_scales[g][:].rearrange("p a k -> p (a k)"),
                     in_=x_grouped[g][:].rearrange("p a k t -> p (a k t)"),
                 )
+            tiles = row_tiles * (H_PASSES if layer == 1 else I_PASSES)
             codes[n] = work.tile([P, CHUNK_TILES * P], U32, name="codes", align_bytes=64)
             scales[n] = work.tile([P, CHUNK_TILES * P], U8, name="scales", align_bytes=64)
             nc.vector.quantize_mx(
-                out=codes[n][:].bitcast(FP8X4),
-                scales=scales[n][:],
-                in_=grouped[n][:].rearrange("p o m t -> p (o m t)"),
+                out=codes[n][:, 0 : tiles * P].bitcast(FP8X4),
+                scales=scales[n][:, 0 : tiles * P],
+                in_=grouped[n][:, 0:tiles, :, :].rearrange("p o m t -> p (o m t)"),
             )
 
         def multiply(n):
-            if not 0 <= n < N_CHUNKS:
+            if not 0 <= n < n_chunks:
                 return
-            layer, g, part = where(n)
-            if layer == 0:
+            layer, g, first_row, row_tiles = chunks[n]
+            if layer == 1:
                 y_bank = sums.tile([P, 4, P], F32, name="y_bank", tag="sum")
-                for t in range(4):
+                for t in range(row_tiles):
                     for a in range(H_PASSES):
                         cols = slice((H_PASSES * t + a) * P, (H_PASSES * t + a + 1) * P)
                         nc.tensor.matmul_mx(
@@ -171,7 +178,7 @@ def tile_dummytemodel_pa_kernel(tc, hf, g1_w, g1_b, g2_w, g2_b, out):
                             stop=(a == H_PASSES - 1),
                         )
                 y_grouped[n] = work.tile([P, P, 4], BF16, name="y_grouped", align_bytes=64)
-                first = 4 * (CHUNKS_PER_GROUP * g + part)
+                first = 4 * (g * I + first_row) // K_PASS
                 nc.vector.tensor_tensor(
                     out=y_grouped[n][:],
                     in0=y_bank[:].rearrange("p t k -> p k t"),
@@ -179,9 +186,10 @@ def tile_dummytemodel_pa_kernel(tc, hf, g1_w, g1_b, g2_w, g2_b, out):
                     op=ADD,
                 )
             else:
-                out_bank = sums.tile([P, W2_ROWS], F32, name="out_bank", tag="sum")
+                width = row_tiles * P
+                out_bank = sums.tile([P, width], F32, name="out_bank", tag="sum")
                 for c in range(I_PASSES):
-                    cols = slice(c * W2_ROWS, (c + 1) * W2_ROWS)
+                    cols = slice(c * width, (c + 1) * width)
                     nc.tensor.matmul_mx(
                         out=out_bank[:],
                         lhsT=y_codes[g][:, c, :].bitcast(FP8X4),
@@ -191,25 +199,25 @@ def tile_dummytemodel_pa_kernel(tc, hf, g1_w, g1_b, g2_w, g2_b, out):
                         start=(c == 0),
                         stop=(c == I_PASSES - 1),
                     )
-                out_sb[n] = work.tile([P, W2_ROWS], F32, name="out_sb")
-                first = part * W2_ROWS
+                out_sb[n] = work.tile([P, width], F32, name="out_sb", tag="out_sb")
                 nc.vector.tensor_tensor(
-                    out=out_sb[n][:], in0=out_bank[:], in1=b2[g][:, first : first + W2_ROWS], op=ADD
+                    out=out_sb[n][:], in0=out_bank[:], in1=b2[g][:, first_row : first_row + width], op=ADD
                 )
 
         def finish(n):
-            if not 0 <= n < N_CHUNKS:
+            if not 0 <= n < n_chunks:
                 return
-            layer, g, part = where(n)
-            if layer == 0:
+            layer, g, first_row, row_tiles = chunks[n]
+            if layer == 1:
+                c = first_row // K_PASS
                 nc.vector.quantize_mx(
-                    out=y_codes[g][:, part, :].bitcast(FP8X4),
-                    scales=y_scales[g][:, part, :],
+                    out=y_codes[g][:, c, :].bitcast(FP8X4),
+                    scales=y_scales[g][:, c, :],
                     in_=y_grouped[n][:].rearrange("p k t -> p (k t)"),
                 )
             else:
                 nc.sync.dma_start(
-                    out=out[g * P : (g + 1) * P, part * W2_ROWS : (part + 1) * W2_ROWS], in_=out_sb[n][:]
+                    out=out[g * P : (g + 1) * P, first_row : first_row + row_tiles * P], in_=out_sb[n][:]
                 )
 
         b1_rows = keep.tile([P, 2 * P], BF16, name="b1_rows")
@@ -219,21 +227,23 @@ def tile_dummytemodel_pa_kernel(tc, hf, g1_w, g1_b, g2_w, g2_b, out):
         n_b1_rows = GROUPS * I // (2 * P)
         nc.sync.dma_start(out=b1_rows[0:n_b1_rows, :], in_=g1_b.rearrange("g (r q) -> (g r) q", q=2 * P))
         nc.sync.dma_start(out=b2_rows[0:GROUPS, :], in_=g2_b)
-        b2 = [keep.tile([P, H], F32, name="b2_%d" % g) for g in range(GROUPS)]
 
-        for n in range(RAW_BUFS - 1):
+        for n in range(RAW_BUFS):
             load(n)
 
         b1_bank = banks.tile([P, P], F32, name="b1_bank", tag="bank")
         nc.tensor.transpose(b1_bank[:], b1_rows[:].bitcast(F32), ident[:])
-        b1_pairs = keep.tile([P, 2 * n_b1_rows], BF16, name="b1_pairs")
-        nc.vector.tensor_copy(out=b1_pairs[:].bitcast(F32), in_=b1_bank[:, 0:n_b1_rows])
-        b1 = keep.tile([P, 2 * n_b1_rows], F32, name="b1")
-        nc.vector.tensor_copy(out=b1[:], in_=b1_pairs[:])
+        b1 = keep.tile([P, 2 * n_b1_rows], BF16, name="b1")
+        nc.vector.tensor_copy(out=b1[:].bitcast(F32), in_=b1_bank[:, 0:n_b1_rows])
 
-        for n in range(N_CHUNKS + 3):
-            finish(n - 3)
-            quantise(n - 1)
-            load(n + RAW_BUFS - 1)
-            flip_chunk(n)
-            multiply(n - 2)
+        for a in range(0, n_chunks + 4, 2):
+            finish(a - 4)
+            finish(a - 3)
+            quantise(a - 1)
+            flip_chunk(a)
+            load(a + RAW_BUFS)
+            quantise(a)
+            flip_chunk(a + 1)
+            load(a + 1 + RAW_BUFS)
+            multiply(a - 2)
+            multiply(a - 1)

@@ -26,7 +26,7 @@ W1_ROWS = I // PARTS
 W2_ROWS = H // PARTS
 CHUNK_TILES = 8
 
-RAW_BUFS = 12
+RAW_BUFS = 6
 VECTOR_EVERY = 8
 
 FLOPS = 2 * GROUPS * P * H * I * 2
@@ -51,6 +51,7 @@ def tile_dummytemodel_pa_kernel(tc, hf, g1_w, g1_b, g2_w, g2_b, out):
         keep = stack.enter_context(tc.tile_pool(name="keep", bufs=1))
         raws = stack.enter_context(tc.tile_pool(name="raws", bufs=RAW_BUFS))
         work = stack.enter_context(tc.tile_pool(name="work", bufs=4))
+        outs = stack.enter_context(tc.tile_pool(name="outs", bufs=2))
         banks = stack.enter_context(tc.psum_pool(name="banks", bufs=6))
         sums = stack.enter_context(tc.psum_pool(name="sums", bufs=2))
         stack.enter_context(tc.manual_schedule())
@@ -67,7 +68,7 @@ def tile_dummytemodel_pa_kernel(tc, hf, g1_w, g1_b, g2_w, g2_b, out):
         codes = {}
         scales = {}
         y_grouped = {}
-        out_sb = {}
+        out_rows = {}
         emptied = []
         x_codes = [keep.tile([P, H_PASSES, P], U32, name="x_codes%d" % g, align_bytes=64) for g in range(GROUPS)]
         x_scales = [keep.tile([P, H_PASSES, P], U8, name="x_scales%d" % g, align_bytes=64) for g in range(GROUPS)]
@@ -199,9 +200,11 @@ def tile_dummytemodel_pa_kernel(tc, hf, g1_w, g1_b, g2_w, g2_b, out):
                         start=(c == 0),
                         stop=(c == I_PASSES - 1),
                     )
-                out_sb[n] = work.tile([P, width], F32, name="out_sb", tag="out_sb")
+                if first_row == 0:
+                    out_rows[g] = outs.tile([P, H], F32, name="out_rows")
+                out_cols = slice(first_row, first_row + width)
                 nc.vector.tensor_tensor(
-                    out=out_sb[n][:], in0=out_bank[:], in1=b2[g][:, first_row : first_row + width], op=ADD
+                    out=out_rows[g][:, out_cols], in0=out_bank[:], in1=b2[g][:, out_cols], op=ADD
                 )
 
         def finish(n):
@@ -215,10 +218,11 @@ def tile_dummytemodel_pa_kernel(tc, hf, g1_w, g1_b, g2_w, g2_b, out):
                     scales=y_scales[g][:, c, :],
                     in_=y_grouped[n][:].rearrange("p k t -> p (k t)"),
                 )
-            else:
-                nc.sync.dma_start(
-                    out=out[g * P : (g + 1) * P, first_row : first_row + row_tiles * P], in_=out_sb[n][:]
-                )
+            elif g == GROUPS - 1:
+                out_cols = slice(first_row, first_row + row_tiles * P)
+                nc.sync.dma_start(out=out[g * P : (g + 1) * P, out_cols], in_=out_rows[g][:, out_cols])
+            elif first_row + row_tiles * P == H:
+                nc.sync.dma_start(out=out[g * P : (g + 1) * P, :], in_=out_rows[g][:])
 
         b1_rows = keep.tile([P, 2 * P], BF16, name="b1_rows")
         nc.vector.memset(b1_rows[:].bitcast(I32), 0)
@@ -236,14 +240,9 @@ def tile_dummytemodel_pa_kernel(tc, hf, g1_w, g1_b, g2_w, g2_b, out):
         b1 = keep.tile([P, 2 * n_b1_rows], BF16, name="b1")
         nc.vector.tensor_copy(out=b1[:].bitcast(F32), in_=b1_bank[:, 0:n_b1_rows])
 
-        for a in range(0, n_chunks + 4, 2):
-            finish(a - 4)
-            finish(a - 3)
-            quantise(a - 1)
-            flip_chunk(a)
-            load(a + RAW_BUFS)
-            quantise(a)
-            flip_chunk(a + 1)
-            load(a + 1 + RAW_BUFS)
-            multiply(a - 2)
-            multiply(a - 1)
+        for n in range(n_chunks + 3):
+            finish(n - 3)
+            quantise(n - 1)
+            flip_chunk(n)
+            load(n + RAW_BUFS)
+            multiply(n - 2)

@@ -51,7 +51,7 @@ def tile_dummytemodel_pa_kernel(tc, hf, g1_w, g1_b, g2_w, g2_b, out):
         keep = stack.enter_context(tc.tile_pool(name="keep", bufs=1))
         raws = stack.enter_context(tc.tile_pool(name="raws", bufs=RAW_BUFS))
         work = stack.enter_context(tc.tile_pool(name="work", bufs=4))
-        outs = stack.enter_context(tc.tile_pool(name="outs", bufs=2))
+        outs = stack.enter_context(tc.tile_pool(name="outs", bufs=GROUPS))
         banks = stack.enter_context(tc.psum_pool(name="banks", bufs=6))
         sums = stack.enter_context(tc.psum_pool(name="sums", bufs=2))
         stack.enter_context(tc.manual_schedule())
@@ -70,6 +70,7 @@ def tile_dummytemodel_pa_kernel(tc, hf, g1_w, g1_b, g2_w, g2_b, out):
         y_grouped = {}
         out_rows = {}
         emptied = []
+        ready = []
         x_codes = [keep.tile([P, H_PASSES, P], U32, name="x_codes%d" % g, align_bytes=64) for g in range(GROUPS)]
         x_scales = [keep.tile([P, H_PASSES, P], U8, name="x_scales%d" % g, align_bytes=64) for g in range(GROUPS)]
         y_codes = [keep.tile([P, I_PASSES, P], U32, name="y_codes%d" % g, align_bytes=64) for g in range(GROUPS)]
@@ -219,10 +220,9 @@ def tile_dummytemodel_pa_kernel(tc, hf, g1_w, g1_b, g2_w, g2_b, out):
                     in_=y_grouped[n][:].rearrange("p k t -> p (k t)"),
                 )
             elif g == GROUPS - 1:
-                out_cols = slice(first_row, first_row + row_tiles * P)
-                nc.sync.dma_start(out=out[g * P : (g + 1) * P, out_cols], in_=out_rows[g][:, out_cols])
+                ready.append((g, first_row, row_tiles * P))
             elif first_row + row_tiles * P == H:
-                nc.sync.dma_start(out=out[g * P : (g + 1) * P, :], in_=out_rows[g][:])
+                ready.append((g, 0, H))
 
         b1_rows = keep.tile([P, 2 * P], BF16, name="b1_rows")
         nc.vector.memset(b1_rows[:].bitcast(I32), 0)
@@ -240,9 +240,15 @@ def tile_dummytemodel_pa_kernel(tc, hf, g1_w, g1_b, g2_w, g2_b, out):
         b1 = keep.tile([P, 2 * n_b1_rows], BF16, name="b1")
         nc.vector.tensor_copy(out=b1[:].bitcast(F32), in_=b1_bank[:, 0:n_b1_rows])
 
-        for n in range(n_chunks + 3):
+        stored = 0
+        for n in range(n_chunks + 4):
             finish(n - 3)
             quantise(n - 1)
             flip_chunk(n)
             load(n + RAW_BUFS)
+            if n + RAW_BUFS >= n_chunks - 1:
+                for g, first_col, width in ready[stored:]:
+                    out_cols = slice(first_col, first_col + width)
+                    nc.sync.dma_start(out=out[g * P : (g + 1) * P, out_cols], in_=out_rows[g][:, out_cols])
+                stored = len(ready)
             multiply(n - 2)

@@ -12,21 +12,27 @@ FP8X4 = mybir.dt.float8_e4m3fn_x4
 ADD = mybir.AluOpType.add
 
 P = 128
+PACK = 4
+HALVES = 2
 GROUPS = 4
 H = 1024
 I = 2048
-K_PASS = 512
+K_PASS = P * PACK
 WORDS_PASS = K_PASS // 2
 H_PASSES = H // K_PASS
 I_PASSES = I // K_PASS
 BANK = 512
+BANK_TILES = BANK // (HALVES * P)
 
 PARTS = 4
 W1_ROWS = I // PARTS
 W2_ROWS = H // PARTS
-CHUNK_TILES = 8
+CHUNK_TILES = W1_ROWS * H // (K_PASS * P)
 
 RAW_BUFS = 6
+WORK_BUFS = 4
+TRANSPOSE_BANKS = 6
+SUM_BANKS = 2
 VECTOR_EVERY = 8
 
 FLOPS = 2 * GROUPS * P * H * I * 2
@@ -43,17 +49,17 @@ def tile_dummytemodel_pa_kernel(tc, hf, g1_w, g1_b, g2_w, g2_b, out):
             if g > 0:
                 pieces = 2 if (g == GROUPS and part == PARTS - 1) else 1
                 for piece in range(pieces):
-                    rows = W2_ROWS // pieces
-                    chunks.append((2, g - 1, part * W2_ROWS + piece * rows, rows // P))
+                    n_rows = W2_ROWS // pieces
+                    chunks.append((2, g - 1, part * W2_ROWS + piece * n_rows, n_rows // P))
     n_chunks = len(chunks)
 
     with ExitStack() as stack:
         keep = stack.enter_context(tc.tile_pool(name="keep", bufs=1))
         raws = stack.enter_context(tc.tile_pool(name="raws", bufs=RAW_BUFS))
-        work = stack.enter_context(tc.tile_pool(name="work", bufs=4))
+        work = stack.enter_context(tc.tile_pool(name="work", bufs=WORK_BUFS))
         outs = stack.enter_context(tc.tile_pool(name="outs", bufs=GROUPS))
-        banks = stack.enter_context(tc.psum_pool(name="banks", bufs=6))
-        sums = stack.enter_context(tc.psum_pool(name="sums", bufs=2))
+        banks = stack.enter_context(tc.psum_pool(name="banks", bufs=TRANSPOSE_BANKS))
+        sums = stack.enter_context(tc.psum_pool(name="sums", bufs=SUM_BANKS))
         stack.enter_context(tc.manual_schedule())
 
         ident = keep.tile([P, P], F32, name="ident")
@@ -86,27 +92,29 @@ def tile_dummytemodel_pa_kernel(tc, hf, g1_w, g1_b, g2_w, g2_b, out):
                     x_raw[g] = raws.tile([P, 1, H], BF16, name="x_raw", tag="x_raw", bufs=2)
                     nc.sync.dma_start(out=x_raw[g][:, 0, :], in_=hf[g * P : (g + 1) * P, :])
                 raw[n] = raws.tile([P, row_tiles, H], BF16, name="raw_w1", tag="raw")
-                rows = g1_w[g, first_row : first_row + W1_ROWS, :]
+                w_rows = g1_w[g, first_row : first_row + W1_ROWS, :]
                 nc.sync.dma_start(
-                    out=raw[n][:].rearrange("p (u e) h -> p u (e h)", u=2),
-                    in_=rows.rearrange("(u p e) h -> p u (e h)", u=2, e=2),
+                    out=raw[n][:].rearrange("p (u e) h -> p u (e h)", u=HALVES),
+                    in_=w_rows.rearrange("(u p e) h -> p u (e h)", u=HALVES, e=2),
                 )
             else:
                 raw[n] = raws.tile([P, row_tiles, I], BF16, name="raw_w2", tag="raw")
-                rows = g2_w[g, first_row : first_row + row_tiles * P, :]
-                nc.sync.dma_start(out=raw[n][:], in_=rows.rearrange("(r p) i -> p r i", p=P))
+                w_rows = g2_w[g, first_row : first_row + row_tiles * P, :]
+                nc.sync.dma_start(out=raw[n][:], in_=w_rows.rearrange("(r p) i -> p r i", p=P))
 
         def flip(raw_tile, operand_tiles, grouped_tile):
             raw_words = raw_tile[:].bitcast(F32)
             grouped_words = grouped_tile[:].bitcast(F32)
-            for b in range(len(operand_tiles) // 2):
-                bank = banks.tile([P, 2, 2, P], F32, name="bank", tag="bank")
-                for x in range(2):
-                    row_tile, k_pass = operand_tiles[2 * b + x]
-                    for u in range(2):
-                        first = WORDS_PASS * k_pass + P * u
-                        nc.tensor.transpose(bank[:, x, u, :], raw_words[:, row_tile, first : first + P], ident[:])
-                dst = grouped_words[:, 2 * b : 2 * b + 2, :, :]
+            for b in range(len(operand_tiles) // BANK_TILES):
+                bank = banks.tile([P, BANK_TILES, HALVES, P], F32, name="bank", tag="bank")
+                for x in range(BANK_TILES):
+                    row_tile, k_pass = operand_tiles[BANK_TILES * b + x]
+                    for u in range(HALVES):
+                        first_word = WORDS_PASS * k_pass + P * u
+                        nc.tensor.transpose(
+                            bank[:, x, u, :], raw_words[:, row_tile, first_word : first_word + P], ident[:]
+                        )
+                dst = grouped_words[:, BANK_TILES * b : BANK_TILES * (b + 1), :, :]
                 src = bank[:].rearrange("p x u m -> p x m u")
                 if len(emptied) % VECTOR_EVERY == VECTOR_EVERY - 1:
                     nc.vector.tensor_copy(out=dst, in_=src)
@@ -132,10 +140,10 @@ def tile_dummytemodel_pa_kernel(tc, hf, g1_w, g1_b, g2_w, g2_b, out):
                 return
             layer, g, first_row, row_tiles = chunks[n]
             if layer == 1 and first_row == 0:
-                x_grouped[g] = work.tile([P, H_PASSES, P, 4], BF16, name="x_grouped", align_bytes=64)
+                x_grouped[g] = work.tile([P, H_PASSES, P, PACK], BF16, name="x_grouped", align_bytes=64)
                 flip(x_raw[g], [(0, a) for a in range(H_PASSES)], x_grouped[g])
                 spread_b2(g)
-            grouped[n] = work.tile([P, CHUNK_TILES, P, 4], BF16, name="grouped", align_bytes=64)
+            grouped[n] = work.tile([P, CHUNK_TILES, P, PACK], BF16, name="grouped", align_bytes=64)
             if layer == 1:
                 operand_tiles = [(t, a) for t in range(row_tiles) for a in range(H_PASSES)]
             else:
@@ -166,7 +174,7 @@ def tile_dummytemodel_pa_kernel(tc, hf, g1_w, g1_b, g2_w, g2_b, out):
                 return
             layer, g, first_row, row_tiles = chunks[n]
             if layer == 1:
-                y_bank = sums.tile([P, 4, P], F32, name="y_bank", tag="sum")
+                y_bank = sums.tile([P, PACK, P], F32, name="y_bank", tag="sum")
                 for t in range(row_tiles):
                     for a in range(H_PASSES):
                         cols = slice((H_PASSES * t + a) * P, (H_PASSES * t + a + 1) * P)
@@ -179,12 +187,12 @@ def tile_dummytemodel_pa_kernel(tc, hf, g1_w, g1_b, g2_w, g2_b, out):
                             start=(a == 0),
                             stop=(a == H_PASSES - 1),
                         )
-                y_grouped[n] = work.tile([P, P, 4], BF16, name="y_grouped", align_bytes=64)
-                first = 4 * (g * I + first_row) // K_PASS
+                y_grouped[n] = work.tile([P, P, PACK], BF16, name="y_grouped", align_bytes=64)
+                first_bias = PACK * (g * I + first_row) // K_PASS
                 nc.vector.tensor_tensor(
                     out=y_grouped[n][:],
                     in0=y_bank[:].rearrange("p t k -> p k t"),
-                    in1=b1[:, first : first + 4].unsqueeze(1).to_broadcast([P, P, 4]),
+                    in1=b1[:, first_bias : first_bias + PACK].unsqueeze(1).to_broadcast([P, P, PACK]),
                     op=ADD,
                 )
             else:
@@ -241,9 +249,9 @@ def tile_dummytemodel_pa_kernel(tc, hf, g1_w, g1_b, g2_w, g2_b, out):
         nc.vector.tensor_copy(out=b1[:].bitcast(F32), in_=b1_bank[:, 0:n_b1_rows])
 
         stored = 0
-        for n in range(n_chunks + 4):
-            finish(n - 3)
+        for n in range(n_chunks + 3):
             quantise(n - 1)
+            finish(n - 3)
             flip_chunk(n)
             load(n + RAW_BUFS)
             if n + RAW_BUFS >= n_chunks - 1:

@@ -100,7 +100,7 @@ def tile_dummytemodel_pa_kernel(tc, hf, g1_w, g1_b, g2_w, g2_b, out):
             else:
                 raw[n] = raws.tile([P, row_tiles, I], BF16, name="raw_w2", tag="raw")
                 w_rows = g2_w[g, first_row : first_row + row_tiles * P, :]
-                nc.sync.dma_start(out=raw[n][:], in_=w_rows.rearrange("(r p) i -> p r i", p=P))
+                nc.sync.dma_start(out=raw[n][:], in_=w_rows.rearrange("(p r) i -> p r i", p=P))
 
         def flip(raw_tile, operand_tiles, grouped_tile):
             raw_words = raw_tile[:].bitcast(F32)
@@ -213,7 +213,10 @@ def tile_dummytemodel_pa_kernel(tc, hf, g1_w, g1_b, g2_w, g2_b, out):
                     out_rows[g] = outs.tile([P, H], F32, name="out_rows")
                 out_cols = slice(first_row, first_row + width)
                 nc.vector.tensor_tensor(
-                    out=out_rows[g][:, out_cols], in0=out_bank[:], in1=b2[g][:, out_cols], op=ADD
+                    out=out_rows[g][:, out_cols].rearrange("k (m r) -> k m r", r=row_tiles),
+                    in0=out_bank[:].rearrange("k (r m) -> k m r", r=row_tiles),
+                    in1=b2[g][:, out_cols].rearrange("k (m r) -> k m r", r=row_tiles),
+                    op=ADD,
                 )
 
         def finish(n):

@@ -88,15 +88,15 @@ def tile_dummytemodel_pa_kernel(tc, hf, g1_w, g1_b, g2_w, g2_b, out):
                 return
             layer, g, first_row, row_tiles = chunks[n]
             if layer == 1:
-                if first_row == 0:
-                    x_raw[g] = raws.tile([P, 1, H], BF16, name="x_raw", tag="x_raw", bufs=2)
-                    nc.sync.dma_start(out=x_raw[g][:, 0, :], in_=hf[g * P : (g + 1) * P, :])
                 raw[n] = raws.tile([P, row_tiles, H], BF16, name="raw_w1", tag="raw")
                 w_rows = g1_w[g, first_row : first_row + W1_ROWS, :]
                 nc.sync.dma_start(
                     out=raw[n][:].rearrange("p (u e) h -> p u (e h)", u=HALVES),
                     in_=w_rows.rearrange("(u p e) h -> p u (e h)", u=HALVES, e=2),
                 )
+                if first_row == 0:
+                    x_raw[g] = raws.tile([P, 1, H], BF16, name="x_raw", tag="x_raw", bufs=2)
+                    nc.sync.dma_start(out=x_raw[g][:, 0, :], in_=hf[g * P : (g + 1) * P, :])
             else:
                 raw[n] = raws.tile([P, row_tiles, I], BF16, name="raw_w2", tag="raw")
                 w_rows = g2_w[g, first_row : first_row + row_tiles * P, :]
@@ -139,27 +139,23 @@ def tile_dummytemodel_pa_kernel(tc, hf, g1_w, g1_b, g2_w, g2_b, out):
             if not 0 <= n < n_chunks:
                 return
             layer, g, first_row, row_tiles = chunks[n]
-            if layer == 1 and first_row == 0:
-                x_grouped[g] = work.tile([P, H_PASSES, P, PACK], BF16, name="x_grouped", align_bytes=64)
-                flip(x_raw[g], [(0, a) for a in range(H_PASSES)], x_grouped[g])
-                spread_b2(g)
             grouped[n] = work.tile([P, CHUNK_TILES, P, PACK], BF16, name="grouped", align_bytes=64)
             if layer == 1:
                 operand_tiles = [(t, a) for t in range(row_tiles) for a in range(H_PASSES)]
             else:
                 operand_tiles = [(r, c) for c in range(I_PASSES) for r in range(row_tiles)]
             flip(raw[n], operand_tiles, grouped[n])
+            if layer == 1 and first_row == 0:
+                x_grouped[g] = work.tile([P, H_PASSES, P, PACK], BF16, name="x_grouped", align_bytes=64)
+                flip(x_raw[g], [(0, a) for a in range(H_PASSES)], x_grouped[g])
+                if g == 0:
+                    flip_b1()
+                spread_b2(g)
 
         def quantise(n):
             if not 0 <= n < n_chunks:
                 return
             layer, g, first_row, row_tiles = chunks[n]
-            if layer == 1 and first_row == 0:
-                nc.vector.quantize_mx(
-                    out=x_codes[g][:].rearrange("p a k -> p (a k)").bitcast(FP8X4),
-                    scales=x_scales[g][:].rearrange("p a k -> p (a k)"),
-                    in_=x_grouped[g][:].rearrange("p a k t -> p (a k t)"),
-                )
             tiles = row_tiles * (H_PASSES if layer == 1 else I_PASSES)
             codes[n] = work.tile([P, CHUNK_TILES * P], U32, name="codes", align_bytes=64)
             scales[n] = work.tile([P, CHUNK_TILES * P], U8, name="scales", align_bytes=64)
@@ -168,6 +164,12 @@ def tile_dummytemodel_pa_kernel(tc, hf, g1_w, g1_b, g2_w, g2_b, out):
                 scales=scales[n][:, 0 : tiles * P],
                 in_=grouped[n][:, 0:tiles, :, :].rearrange("p o m t -> p (o m t)"),
             )
+            if layer == 1 and first_row == 0:
+                nc.vector.quantize_mx(
+                    out=x_codes[g][:].rearrange("p a k -> p (a k)").bitcast(FP8X4),
+                    scales=x_scales[g][:].rearrange("p a k -> p (a k)"),
+                    in_=x_grouped[g][:].rearrange("p a k t -> p (a k t)"),
+                )
 
         def multiply(n):
             if not 0 <= n < n_chunks:
@@ -240,16 +242,18 @@ def tile_dummytemodel_pa_kernel(tc, hf, g1_w, g1_b, g2_w, g2_b, out):
         b2_rows = keep.tile([P, H], BF16, name="b2_rows")
         nc.vector.memset(b2_rows[:].bitcast(I32), 0)
         n_b1_rows = GROUPS * I // (2 * P)
+        load(0)
         nc.sync.dma_start(out=b1_rows[0:n_b1_rows, :], in_=g1_b.rearrange("g (r q) -> (g r) q", q=2 * P))
         nc.sync.dma_start(out=b2_rows[0:GROUPS, :], in_=g2_b)
-
-        for n in range(RAW_BUFS):
+        for n in range(1, RAW_BUFS):
             load(n)
 
-        b1_bank = banks.tile([P, P], F32, name="b1_bank", tag="bank")
-        nc.tensor.transpose(b1_bank[:], b1_rows[:].bitcast(F32), ident[:])
         b1 = keep.tile([P, 2 * n_b1_rows], BF16, name="b1")
-        nc.vector.tensor_copy(out=b1[:].bitcast(F32), in_=b1_bank[:, 0:n_b1_rows])
+
+        def flip_b1():
+            b1_bank = banks.tile([P, P], F32, name="b1_bank", tag="bank")
+            nc.tensor.transpose(b1_bank[:], b1_rows[:].bitcast(F32), ident[:])
+            nc.vector.tensor_copy(out=b1[:].bitcast(F32), in_=b1_bank[:, 0:n_b1_rows])
 
         stored = 0
         for n in range(n_chunks + 3):

@@ -28,38 +28,75 @@ PARTS = 4
 W1_ROWS = I // PARTS
 W2_ROWS = H // PARTS
 CHUNK_TILES = W1_ROWS * H // (K_PASS * P)
-
-RAW_BUFS = 6
-WORK_BUFS = 4
-TRANSPOSE_BANKS = 6
-SUM_BANKS = 2
-VECTOR_EVERY = 8
-
+CHUNK_COLS = W1_ROWS * H // P
 FLOPS = 2 * GROUPS * P * H * I * 2
+
+CFG = {"order":"alt","load_mid":1,"load_head":2,"load_tail":3,"round_mid":1,"round_head":4,"round_tail":4,"raw_kib":48,"work_bufs":4,"vector_every":8,"t_banks":6,"sum_banks":2,"bias_q":"sync_second","c0_split":2,"x_after":1,"spread":"group","tail":"rows2","lagq":1,"lagm":2,"lagf":3,"tailcopy":0}
 
 
 def tile_dummytemodel_pa_kernel(tc, hf, g1_w, g1_b, g2_w, g2_b, out):
     nc = tc.nc
-
+    C = CFG
+    VECTOR_EVERY = C['vector_every']
+    def l2_chunks(g, part, last):
+        ts = C.get('tailspec', {})
+        if g == GROUPS - 1 and str(part) in ts:
+            return [(2, g, part * W2_ROWS + 128 * ro, rt, fp_, np_) for ro, rt, fp_, np_ in ts[str(part)]]
+        if not last:
+            return [(2, g, part * W2_ROWS, 2, 0, 4)]
+        if C['tail'] == 'rows2':
+            return [(2, g, part * W2_ROWS + 128 * i, 1, 0, 4) for i in range(2)]
+        if C['tail'] == 'k4':
+            return [(2, g, part * W2_ROWS, 2, c, 1) for c in range(4)]
+        if C['tail'] == 'k2':
+            return [(2, g, part * W2_ROWS, 2, 2 * c, 2) for c in range(2)]
+        if C['tail'] == 'k211':
+            return [(2, g, part * W2_ROWS, 2, 0, 2), (2, g, part * W2_ROWS, 2, 2, 1), (2, g, part * W2_ROWS, 2, 3, 1)]
+        if C['tail'] == 'rows2k2':
+            return [(2, g, part * W2_ROWS, 1, 0, 4), (2, g, part * W2_ROWS + 128, 1, 0, 2), (2, g, part * W2_ROWS + 128, 1, 2, 2)]
+        if C['tail'] == 'none':
+            return [(2, g, part * W2_ROWS, 2, 0, 4)]
     chunks = []
+    step = 1 if C['order'] == 'alt' else 2
     for g in range(GROUPS + 1):
-        for part in range(PARTS):
+        for fp in range(0, PARTS, step):
             if g < GROUPS:
-                chunks.append((1, g, part * W1_ROWS, W1_ROWS // P))
+                for part in range(fp, fp + step):
+                    chunks.append((1, g, part * W1_ROWS, 4, 0, 2))
             if g > 0:
-                pieces = 2 if (g == GROUPS and part == PARTS - 1) else 1
-                for piece in range(pieces):
-                    n_rows = W2_ROWS // pieces
-                    chunks.append((2, g - 1, part * W2_ROWS + piece * n_rows, n_rows // P))
+                for part in range(fp, fp + step):
+                    chunks.extend(l2_chunks(g - 1, part, g == GROUPS and part == PARTS - 1))
     n_chunks = len(chunks)
+    full = lambda n: chunks[n][3] * chunks[n][5] == 8
+    loads = []
+    for n in range(n_chunks):
+        alone = n < C['load_head'] or n >= n_chunks - C['load_tail'] or not full(n) or n >= C.get('load_until', 999)
+        if (not alone and loads and len(loads[-1]) < C['load_mid'] and loads[-1][0] >= C['load_head']
+                and chunks[loads[-1][0]][0:2] == chunks[n][0:2] and chunks[loads[-1][-1]][2] + chunks[n][3] * P == chunks[n][2]):
+            loads[-1].append(n)
+        else:
+            loads.append([n])
+    load_of = {}
+    for j, members in enumerate(loads):
+        for place, n in enumerate(members):
+            load_of[n] = (j, place)
+    rounds = []
+    n = 0
+    while n < n_chunks:
+        size = 1 if (n < C['round_head'] or n >= n_chunks - C['round_tail']) else C['round_mid']
+        if n == n_chunks - C.get('last_round', 0):
+            size = C['last_round']
+        rounds.append(list(range(n, min(n + size, n_chunks))))
+        n += size
+    RAW_BUFS = C['raw_kib'] // (8 * C['load_mid'])
 
     with ExitStack() as stack:
         keep = stack.enter_context(tc.tile_pool(name="keep", bufs=1))
         raws = stack.enter_context(tc.tile_pool(name="raws", bufs=RAW_BUFS))
-        work = stack.enter_context(tc.tile_pool(name="work", bufs=WORK_BUFS))
+        work = stack.enter_context(tc.tile_pool(name="work", bufs=C['work_bufs']))
         outs = stack.enter_context(tc.tile_pool(name="outs", bufs=GROUPS))
-        banks = stack.enter_context(tc.psum_pool(name="banks", bufs=TRANSPOSE_BANKS))
-        sums = stack.enter_context(tc.psum_pool(name="sums", bufs=SUM_BANKS))
+        banks = stack.enter_context(tc.psum_pool(name="banks", bufs=C['t_banks']))
+        sums = stack.enter_context(tc.psum_pool(name="sums", bufs=C['sum_banks']))
         stack.enter_context(tc.manual_schedule())
 
         ident = keep.tile([P, P], F32, name="ident")
@@ -67,96 +104,130 @@ def tile_dummytemodel_pa_kernel(tc, hf, g1_w, g1_b, g2_w, g2_b, out):
         ident_bf = keep.tile([P, P], BF16, name="ident_bf")
         make_identity(nc, ident_bf[:])
 
-        raw = {}
-        x_raw = {}
-        grouped = {}
-        x_grouped = {}
-        codes = {}
-        scales = {}
-        y_grouped = {}
-        out_rows = {}
-        emptied = []
-        ready = []
+        raw, issued, x_raw, grouped, x_grouped, codes, scales, y_grouped, out_rows, out_banks = {}, [], {}, {}, {}, {}, {}, {}, {}, {}
+        emptied, ready, tail_emptied = [], [], []
         x_codes = [keep.tile([P, H_PASSES, P], U32, name="x_codes%d" % g, align_bytes=64) for g in range(GROUPS)]
         x_scales = [keep.tile([P, H_PASSES, P], U8, name="x_scales%d" % g, align_bytes=64) for g in range(GROUPS)]
         y_codes = [keep.tile([P, I_PASSES, P], U32, name="y_codes%d" % g, align_bytes=64) for g in range(GROUPS)]
         y_scales = [keep.tile([P, I_PASSES, P], U8, name="y_scales%d" % g, align_bytes=64) for g in range(GROUPS)]
         b2 = [keep.tile([P, H], BF16, name="b2_%d" % g) for g in range(GROUPS)]
 
-        def load(n):
-            if not 0 <= n < n_chunks:
-                return
-            layer, g, first_row, row_tiles = chunks[n]
-            if layer == 1:
-                raw[n] = raws.tile([P, row_tiles, H], BF16, name="raw_w1", tag="raw")
-                w_rows = g1_w[g, first_row : first_row + W1_ROWS, :]
-                nc.sync.dma_start(
-                    out=raw[n][:].rearrange("p (u e) h -> p u (e h)", u=HALVES),
-                    in_=w_rows.rearrange("(u p e) h -> p u (e h)", u=HALVES, e=2),
-                )
-                if first_row == 0:
-                    x_raw[g] = raws.tile([P, 1, H], BF16, name="x_raw", tag="x_raw", bufs=2)
-                    nc.sync.dma_start(out=x_raw[g][:, 0, :], in_=hf[g * P : (g + 1) * P, :])
-            else:
-                raw[n] = raws.tile([P, row_tiles, I], BF16, name="raw_w2", tag="raw")
-                w_rows = g2_w[g, first_row : first_row + row_tiles * P, :]
-                nc.sync.dma_start(out=raw[n][:], in_=w_rows.rearrange("(p r) i -> p r i", p=P))
+        if C.get('xall'):
+            xa_raw = keep.tile([P, GROUPS, H], BF16, name="xa_raw")
+            xa_grouped = keep.tile([P, GROUPS * H_PASSES, P, PACK], BF16, name="xa_grouped", align_bytes=64)
+            xa_codes = keep.tile([P, GROUPS, H_PASSES, P], U32, name="xa_codes", align_bytes=64)
+            xa_scales = keep.tile([P, GROUPS, H_PASSES, P], U8, name="xa_scales", align_bytes=64)
 
-        def flip(raw_tile, operand_tiles, grouped_tile):
-            raw_words = raw_tile[:].bitcast(F32)
+        def load_x(g):
+            if C.get('xall'):
+                return
+            x_raw[g] = raws.tile([P, 1, H], BF16, name="x_raw", tag="x_raw", bufs=2)
+            nc.sync.dma_start(out=x_raw[g][:, 0, :], in_=hf[g * P : (g + 1) * P, :])
+
+        def load(j):
+            if not 0 <= j < len(loads):
+                return
+            issued.append(j)
+            layer, g, first_row, row_tiles, first_pass, n_passes = chunks[loads[j][0]]
+            n_members = len(loads[j])
+            raw[j] = raws.tile([P, C['load_mid'] * CHUNK_COLS], BF16, name="raw", tag="raw")
+            if layer == 1:
+                if first_row == 0 and not C['x_after']:
+                    load_x(g)
+                w_rows = g1_w[g, first_row : first_row + n_members * W1_ROWS, :]
+                split = C['c0_split'] if j == 0 else 1
+                per = n_members * 2 // split
+                for s in range(split):
+                    nc.sync.dma_start(
+                        out=raw[j][:, s * per * 2 * H : (s + 1) * per * 2 * H].rearrange("p (u q) -> p u q", q=2 * H),
+                        in_=w_rows[s * per * 256 : (s + 1) * per * 256, :].rearrange("(u p e) h -> p u (e h)", p=P, e=2),
+                    )
+                if first_row == 0 and C['x_after']:
+                    load_x(g)
+            else:
+                w_rows = g2_w[g, first_row : first_row + n_members * row_tiles * P, first_pass * K_PASS : (first_pass + n_passes) * K_PASS]
+                nc.sync.dma_start(
+                    out=raw[j][:, 0 : n_members * row_tiles * n_passes * K_PASS].rearrange("p (c q) -> p c q", c=n_members * row_tiles),
+                    in_=w_rows.rearrange("(c p r) i -> p (c r) i", c=n_members, p=P),
+                )
+
+        def flip(raw_rows, operand_tiles, grouped_tile, tailcopy=False):
+            raw_words = raw_rows.bitcast(F32)
             grouped_words = grouped_tile[:].bitcast(F32)
-            for b in range(len(operand_tiles) // BANK_TILES):
+            nb = (len(operand_tiles) + BANK_TILES - 1) // BANK_TILES
+            for b in range(nb):
+                tiles = operand_tiles[BANK_TILES * b : BANK_TILES * (b + 1)]
                 bank = banks.tile([P, BANK_TILES, HALVES, P], F32, name="bank", tag="bank")
-                for x in range(BANK_TILES):
-                    row_tile, k_pass = operand_tiles[BANK_TILES * b + x]
+                for x, (row_tile, k_pass) in enumerate(tiles):
                     for u in range(HALVES):
                         first_word = WORDS_PASS * k_pass + P * u
-                        nc.tensor.transpose(
-                            bank[:, x, u, :], raw_words[:, row_tile, first_word : first_word + P], ident[:]
-                        )
-                dst = grouped_words[:, BANK_TILES * b : BANK_TILES * (b + 1), :, :]
-                src = bank[:].rearrange("p x u m -> p x m u")
-                if len(emptied) % VECTOR_EVERY == VECTOR_EVERY - 1:
+                        nc.tensor.transpose(bank[:, x, u, :], raw_words[:, row_tile, first_word : first_word + P], ident[:])
+                dst = grouped_words[:, BANK_TILES * b : BANK_TILES * b + len(tiles), :, :]
+                src = bank[:, 0 : len(tiles), :, :].rearrange("p x u m -> p x m u")
+                if tailcopy:
+                    tail_emptied.append(b)
+                    onv = len(tail_emptied) % C.get('tail_mod', 2) == 0
+                else:
+                    onv = len(emptied) % VECTOR_EVERY == VECTOR_EVERY - 1
+                    emptied.append(b)
+                if onv:
                     nc.vector.tensor_copy(out=dst, in_=src)
                 else:
                     nc.scalar.copy(out=dst, in_=src)
-                emptied.append(b)
 
         def spread_b2(g):
             b2_bank = banks.tile([P, H], BF16, name="b2_bank", tag="bank")
             for half in range(H // BANK):
                 cols = slice(half * BANK, (half + 1) * BANK)
-                nc.tensor.matmul(
-                    out=b2_bank[:, cols],
-                    lhsT=ident_bf[:, g : g + 1].to_broadcast([P, P]),
-                    rhs=b2_rows[:, cols],
-                    start=True,
-                    stop=True,
-                )
-            nc.scalar.copy(out=b2[g][:], in_=b2_bank[:])
+                nc.tensor.matmul(out=b2_bank[:, cols], lhsT=ident_bf[:, g : g + 1].to_broadcast([P, P]), rhs=b2_rows[:, cols], start=True, stop=True)
+            (nc.vector.tensor_copy if C.get('xall') else nc.scalar.copy)(out=b2[g][:], in_=b2_bank[:])
+
+        def flip_x(g):
+            if C.get('xall'):
+                return
+            x_grouped[g] = work.tile([P, H_PASSES, P, PACK], BF16, name="x_grouped", align_bytes=64)
+            flip(x_raw[g][:], [(0, a) for a in range(H_PASSES)], x_grouped[g])
 
         def flip_chunk(n):
             if not 0 <= n < n_chunks:
                 return
-            layer, g, first_row, row_tiles = chunks[n]
+            layer, g, first_row, row_tiles, first_pass, n_passes = chunks[n]
+            first = layer == 1 and first_row == 0
+            if first and not C['x_after']:
+                flip_x(g)
+                if C['spread'] == 'group':
+                    spread_b2(g)
             grouped[n] = work.tile([P, CHUNK_TILES, P, PACK], BF16, name="grouped", align_bytes=64)
             if layer == 1:
                 operand_tiles = [(t, a) for t in range(row_tiles) for a in range(H_PASSES)]
             else:
-                operand_tiles = [(r, c) for c in range(I_PASSES) for r in range(row_tiles)]
-            flip(raw[n], operand_tiles, grouped[n])
-            if layer == 1 and first_row == 0:
-                x_grouped[g] = work.tile([P, H_PASSES, P, PACK], BF16, name="x_grouped", align_bytes=64)
-                flip(x_raw[g], [(0, a) for a in range(H_PASSES)], x_grouped[g])
-                if g == 0:
-                    flip_b1()
-                spread_b2(g)
+                operand_tiles = [(r, c) for c in range(n_passes) for r in range(row_tiles)]
+            j, place = load_of[n]
+            chunk_cols = slice(place * CHUNK_COLS, place * CHUNK_COLS + row_tiles * n_passes * K_PASS)
+            flip(raw[j][:, chunk_cols].rearrange("p (t k) -> p t k", t=row_tiles), operand_tiles, grouped[n], tailcopy=(C['tailcopy'] and n >= n_chunks - C['tailcopy']))
+            if first and C['x_after']:
+                flip_x(g)
+                if n == 0:
+                    head_work()
+                if C['spread'] == 'group':
+                    spread_b2(g)
+            if n == loads[j][-1]:
+                load(j + RAW_BUFS)
 
         def quantise(n):
             if not 0 <= n < n_chunks:
                 return
-            layer, g, first_row, row_tiles = chunks[n]
-            tiles = row_tiles * (H_PASSES if layer == 1 else I_PASSES)
+            layer, g, first_row, row_tiles, first_pass, n_passes = chunks[n]
+            def quantise_x():
+                if layer == 1 and first_row == 0 and not C.get('xall'):
+                    nc.vector.quantize_mx(
+                        out=x_codes[g][:].rearrange("p a k -> p (a k)").bitcast(FP8X4),
+                        scales=x_scales[g][:].rearrange("p a k -> p (a k)"),
+                        in_=x_grouped[g][:].rearrange("p a k t -> p (a k t)"),
+                    )
+            if not C['x_after']:
+                quantise_x()
+            tiles = row_tiles * n_passes
             codes[n] = work.tile([P, CHUNK_TILES * P], U32, name="codes", align_bytes=64)
             scales[n] = work.tile([P, CHUNK_TILES * P], U8, name="scales", align_bytes=64)
             nc.vector.quantize_mx(
@@ -164,74 +235,62 @@ def tile_dummytemodel_pa_kernel(tc, hf, g1_w, g1_b, g2_w, g2_b, out):
                 scales=scales[n][:, 0 : tiles * P],
                 in_=grouped[n][:, 0:tiles, :, :].rearrange("p o m t -> p (o m t)"),
             )
-            if layer == 1 and first_row == 0:
-                nc.vector.quantize_mx(
-                    out=x_codes[g][:].rearrange("p a k -> p (a k)").bitcast(FP8X4),
-                    scales=x_scales[g][:].rearrange("p a k -> p (a k)"),
-                    in_=x_grouped[g][:].rearrange("p a k t -> p (a k t)"),
-                )
+            if C['x_after']:
+                quantise_x()
 
         def multiply(n):
             if not 0 <= n < n_chunks:
                 return
-            layer, g, first_row, row_tiles = chunks[n]
+            layer, g, first_row, row_tiles, first_pass, n_passes = chunks[n]
             if layer == 1:
                 y_bank = sums.tile([P, PACK, P], F32, name="y_bank", tag="sum")
                 for t in range(row_tiles):
                     for a in range(H_PASSES):
                         cols = slice((H_PASSES * t + a) * P, (H_PASSES * t + a + 1) * P)
                         nc.tensor.matmul_mx(
-                            out=y_bank[:, t, :],
-                            lhsT=codes[n][:, cols].bitcast(FP8X4),
-                            lhsT_scale=scales[n][:, cols],
-                            rhs=x_codes[g][:, a, :].bitcast(FP8X4),
-                            rhs_scale=x_scales[g][:, a, :],
-                            start=(a == 0),
-                            stop=(a == H_PASSES - 1),
+                            out=y_bank[:, t, :], lhsT=codes[n][:, cols].bitcast(FP8X4), lhsT_scale=scales[n][:, cols],
+                            rhs=(xa_codes[:, g, a, :] if C.get('xall') else x_codes[g][:, a, :]).bitcast(FP8X4), rhs_scale=(xa_scales[:, g, a, :] if C.get('xall') else x_scales[g][:, a, :]),
+                            start=(a == 0), stop=(a == H_PASSES - 1),
                         )
                 y_grouped[n] = work.tile([P, P, PACK], BF16, name="y_grouped", align_bytes=64)
                 first_bias = PACK * (g * I + first_row) // K_PASS
                 nc.vector.tensor_tensor(
-                    out=y_grouped[n][:],
-                    in0=y_bank[:].rearrange("p t k -> p k t"),
-                    in1=b1[:, first_bias : first_bias + PACK].unsqueeze(1).to_broadcast([P, P, PACK]),
-                    op=ADD,
+                    out=y_grouped[n][:], in0=y_bank[:].rearrange("p t k -> p k t"),
+                    in1=b1[:, first_bias : first_bias + PACK].unsqueeze(1).to_broadcast([P, P, PACK]), op=ADD,
                 )
             else:
                 width = row_tiles * P
-                out_bank = sums.tile([P, width], F32, name="out_bank", tag="sum")
-                for c in range(I_PASSES):
+                if first_pass == 0:
+                    out_banks[(g, first_row)] = sums.tile([P, width], F32, name="out_bank", tag="sum")
+                out_bank = out_banks[(g, first_row)]
+                for c in range(n_passes):
                     cols = slice(c * width, (c + 1) * width)
+                    cc = first_pass + c
                     nc.tensor.matmul_mx(
-                        out=out_bank[:],
-                        lhsT=y_codes[g][:, c, :].bitcast(FP8X4),
-                        lhsT_scale=y_scales[g][:, c, :],
-                        rhs=codes[n][:, cols].bitcast(FP8X4),
-                        rhs_scale=scales[n][:, cols],
-                        start=(c == 0),
-                        stop=(c == I_PASSES - 1),
+                        out=out_bank[:], lhsT=y_codes[g][:, cc, :].bitcast(FP8X4), lhsT_scale=y_scales[g][:, cc, :],
+                        rhs=codes[n][:, cols].bitcast(FP8X4), rhs_scale=scales[n][:, cols],
+                        start=(cc == 0), stop=(cc == I_PASSES - 1),
                     )
+                if first_pass + n_passes < I_PASSES:
+                    return
                 if first_row == 0:
                     out_rows[g] = outs.tile([P, H], F32, name="out_rows")
                 out_cols = slice(first_row, first_row + width)
                 nc.vector.tensor_tensor(
                     out=out_rows[g][:, out_cols].rearrange("k (m r) -> k m r", r=row_tiles),
                     in0=out_bank[:].rearrange("k (r m) -> k m r", r=row_tiles),
-                    in1=b2[g][:, out_cols].rearrange("k (m r) -> k m r", r=row_tiles),
-                    op=ADD,
+                    in1=b2[g][:, out_cols].rearrange("k (m r) -> k m r", r=row_tiles), op=ADD,
                 )
 
         def finish(n):
             if not 0 <= n < n_chunks:
                 return
-            layer, g, first_row, row_tiles = chunks[n]
+            layer, g, first_row, row_tiles, first_pass, n_passes = chunks[n]
             if layer == 1:
                 c = first_row // K_PASS
-                nc.vector.quantize_mx(
-                    out=y_codes[g][:, c, :].bitcast(FP8X4),
-                    scales=y_scales[g][:, c, :],
-                    in_=y_grouped[n][:].rearrange("p k t -> p (k t)"),
-                )
+                nc.vector.quantize_mx(out=y_codes[g][:, c, :].bitcast(FP8X4), scales=y_scales[g][:, c, :], in_=y_grouped[n][:].rearrange("p k t -> p (k t)"))
+            elif first_pass + n_passes < I_PASSES:
+                return
             elif g == GROUPS - 1:
                 ready.append((g, first_row, row_tiles * P))
             elif first_row + row_tiles * P == H:
@@ -242,28 +301,51 @@ def tile_dummytemodel_pa_kernel(tc, hf, g1_w, g1_b, g2_w, g2_b, out):
         b2_rows = keep.tile([P, H], BF16, name="b2_rows")
         nc.vector.memset(b2_rows[:].bitcast(I32), 0)
         n_b1_rows = GROUPS * I // (2 * P)
+        def bias_loads(q):
+            q.dma_start(out=b1_rows[0:n_b1_rows, :], in_=g1_b.rearrange("g (r q) -> (g r) q", q=2 * P))
+            q.dma_start(out=b2_rows[0:GROUPS, :], in_=g2_b)
+        if C['bias_q'] == 'sync_first':
+            bias_loads(nc.sync)
+        elif C['bias_q'] == 'scalar':
+            bias_loads(nc.scalar)
+        if C.get('xall'):
+            nc.sync.dma_start(out=xa_raw[:], in_=hf.rearrange("(g p) h -> p g h", p=P))
         load(0)
-        nc.sync.dma_start(out=b1_rows[0:n_b1_rows, :], in_=g1_b.rearrange("g (r q) -> (g r) q", q=2 * P))
-        nc.sync.dma_start(out=b2_rows[0:GROUPS, :], in_=g2_b)
-        for n in range(1, RAW_BUFS):
-            load(n)
+        if C['bias_q'] == 'sync_second':
+            bias_loads(nc.sync)
+        for j in range(1, RAW_BUFS):
+            load(j)
 
         b1 = keep.tile([P, 2 * n_b1_rows], BF16, name="b1")
-
-        def flip_b1():
+        def head_work():
             b1_bank = banks.tile([P, P], F32, name="b1_bank", tag="bank")
             nc.tensor.transpose(b1_bank[:], b1_rows[:].bitcast(F32), ident[:])
             nc.vector.tensor_copy(out=b1[:].bitcast(F32), in_=b1_bank[:, 0:n_b1_rows])
+            if C['spread'] == 'head':
+                for g in range(GROUPS):
+                    spread_b2(g)
+        if not C['x_after']:
+            head_work()
+        if C.get('xall'):
+            flip(xa_raw[:], [(g, a) for g in range(GROUPS) for a in range(H_PASSES)], xa_grouped)
 
         stored = 0
-        for n in range(n_chunks + 3):
-            quantise(n - 1)
-            finish(n - 3)
-            flip_chunk(n)
-            load(n + RAW_BUFS)
-            if n + RAW_BUFS >= n_chunks - 1:
+        R = lambda r: rounds[r] if 0 <= r < len(rounds) else []
+        for r in range(len(rounds) + C['lagf']):
+            if r == 1 and C.get('xall'):
+                nc.vector.quantize_mx(out=xa_codes[:].rearrange("p g a k -> p (g a k)").bitcast(FP8X4), scales=xa_scales[:].rearrange("p g a k -> p (g a k)"), in_=xa_grouped[:].rearrange("p o k t -> p (o k t)"))
+            qs, fs = R(r - C['lagq']), R(r - C['lagf'])
+            for i in range(max(len(qs), len(fs))):
+                if i < len(qs):
+                    quantise(qs[i])
+                if i < len(fs):
+                    finish(fs[i])
+            for n in R(r):
+                flip_chunk(n)
+            if len(issued) == len(loads):
                 for g, first_col, width in ready[stored:]:
                     out_cols = slice(first_col, first_col + width)
                     nc.sync.dma_start(out=out[g * P : (g + 1) * P, out_cols], in_=out_rows[g][:, out_cols])
                 stored = len(ready)
-            multiply(n - 2)
+            for n in R(r - C['lagm']):
+                multiply(n)

from contextlib import ExitStack

import concourse.mybir as mybir
from concourse.masks import make_identity

BF16 = mybir.dt.bfloat16
F32 = mybir.dt.float32
I32 = mybir.dt.int32
U32 = mybir.dt.uint32
U8 = mybir.dt.uint8
FP8X4 = mybir.dt.float8_e4m3fn_x4
ADD = mybir.AluOpType.add

P = 128
PACK = 4
HALVES = 2
GROUPS = 4
H = 1024
I = 2048
K_PASS = P * PACK
WORDS_PASS = K_PASS // 2
H_PASSES = H // K_PASS
I_PASSES = I // K_PASS
BANK = 512
BANK_TILES = BANK // (HALVES * P)

PARTS = 4
W1_ROWS = I // PARTS
W2_ROWS = H // PARTS
CHUNK_TILES = W1_ROWS * H // (K_PASS * P)
CHUNK_COLS = W1_ROWS * H // P
FLOPS = 2 * GROUPS * P * H * I * 2

CFG = {"order":"alt","load_mid":1,"load_head":2,"load_tail":3,"round_mid":1,"round_head":4,"round_tail":4,"raw_kib":48,"work_bufs":4,"vector_every":8,"t_banks":6,"sum_banks":2,"bias_q":"sync_second","c0_split":2,"x_after":1,"spread":"group","tail":"rows2","lagq":1,"lagm":2,"lagf":3,"tailcopy":0}


def tile_dummytemodel_pa_kernel(tc, hf, g1_w, g1_b, g2_w, g2_b, out):
    nc = tc.nc
    C = CFG
    VECTOR_EVERY = C['vector_every']
    def l2_chunks(g, part, last):
        ts = C.get('tailspec', {})
        if g == GROUPS - 1 and str(part) in ts:
            return [(2, g, part * W2_ROWS + 128 * ro, rt, fp_, np_) for ro, rt, fp_, np_ in ts[str(part)]]
        if not last:
            return [(2, g, part * W2_ROWS, 2, 0, 4)]
        if C['tail'] == 'rows2':
            return [(2, g, part * W2_ROWS + 128 * i, 1, 0, 4) for i in range(2)]
        if C['tail'] == 'k4':
            return [(2, g, part * W2_ROWS, 2, c, 1) for c in range(4)]
        if C['tail'] == 'k2':
            return [(2, g, part * W2_ROWS, 2, 2 * c, 2) for c in range(2)]
        if C['tail'] == 'k211':
            return [(2, g, part * W2_ROWS, 2, 0, 2), (2, g, part * W2_ROWS, 2, 2, 1), (2, g, part * W2_ROWS, 2, 3, 1)]
        if C['tail'] == 'rows2k2':
            return [(2, g, part * W2_ROWS, 1, 0, 4), (2, g, part * W2_ROWS + 128, 1, 0, 2), (2, g, part * W2_ROWS + 128, 1, 2, 2)]
        if C['tail'] == 'none':
            return [(2, g, part * W2_ROWS, 2, 0, 4)]
    chunks = []
    step = 1 if C['order'] == 'alt' else 2
    for g in range(GROUPS + 1):
        for fp in range(0, PARTS, step):
            if g < GROUPS:
                for part in range(fp, fp + step):
                    chunks.append((1, g, part * W1_ROWS, 4, 0, 2))
            if g > 0:
                for part in range(fp, fp + step):
                    chunks.extend(l2_chunks(g - 1, part, g == GROUPS and part == PARTS - 1))
    n_chunks = len(chunks)
    full = lambda n: chunks[n][3] * chunks[n][5] == 8
    loads = []
    for n in range(n_chunks):
        alone = n < C['load_head'] or n >= n_chunks - C['load_tail'] or not full(n) or n >= C.get('load_until', 999)
        if (not alone and loads and len(loads[-1]) < C['load_mid'] and loads[-1][0] >= C['load_head']
                and chunks[loads[-1][0]][0:2] == chunks[n][0:2] and chunks[loads[-1][-1]][2] + chunks[n][3] * P == chunks[n][2]):
            loads[-1].append(n)
        else:
            loads.append([n])
    load_of = {}
    for j, members in enumerate(loads):
        for place, n in enumerate(members):
            load_of[n] = (j, place)
    rounds = []
    n = 0
    while n < n_chunks:
        size = 1 if (n < C['round_head'] or n >= n_chunks - C['round_tail']) else C['round_mid']
        if n == n_chunks - C.get('last_round', 0):
            size = C['last_round']
        rounds.append(list(range(n, min(n + size, n_chunks))))
        n += size
    RAW_BUFS = C['raw_kib'] // (8 * C['load_mid'])

    with ExitStack() as stack:
        keep = stack.enter_context(tc.tile_pool(name="keep", bufs=1))
        raws = stack.enter_context(tc.tile_pool(name="raws", bufs=RAW_BUFS))
        work = stack.enter_context(tc.tile_pool(name="work", bufs=C['work_bufs']))
        outs = stack.enter_context(tc.tile_pool(name="outs", bufs=GROUPS))
        banks = stack.enter_context(tc.psum_pool(name="banks", bufs=C['t_banks']))
        sums = stack.enter_context(tc.psum_pool(name="sums", bufs=C['sum_banks']))
        stack.enter_context(tc.manual_schedule())

        ident = keep.tile([P, P], F32, name="ident")
        make_identity(nc, ident[:])
        ident_bf = keep.tile([P, P], BF16, name="ident_bf")
        make_identity(nc, ident_bf[:])

        raw, issued, x_raw, grouped, x_grouped, codes, scales, y_grouped, out_rows, out_banks = {}, [], {}, {}, {}, {}, {}, {}, {}, {}
        emptied, ready, tail_emptied = [], [], []
        x_codes = [keep.tile([P, H_PASSES, P], U32, name="x_codes%d" % g, align_bytes=64) for g in range(GROUPS)]
        x_scales = [keep.tile([P, H_PASSES, P], U8, name="x_scales%d" % g, align_bytes=64) for g in range(GROUPS)]
        y_codes = [keep.tile([P, I_PASSES, P], U32, name="y_codes%d" % g, align_bytes=64) for g in range(GROUPS)]
        y_scales = [keep.tile([P, I_PASSES, P], U8, name="y_scales%d" % g, align_bytes=64) for g in range(GROUPS)]
        b2 = [keep.tile([P, H], BF16, name="b2_%d" % g) for g in range(GROUPS)]

        if C.get('xall'):
            xa_raw = keep.tile([P, GROUPS, H], BF16, name="xa_raw")
            xa_grouped = keep.tile([P, GROUPS * H_PASSES, P, PACK], BF16, name="xa_grouped", align_bytes=64)
            xa_codes = keep.tile([P, GROUPS, H_PASSES, P], U32, name="xa_codes", align_bytes=64)
            xa_scales = keep.tile([P, GROUPS, H_PASSES, P], U8, name="xa_scales", align_bytes=64)

        def load_x(g):
            if C.get('xall'):
                return
            x_raw[g] = raws.tile([P, 1, H], BF16, name="x_raw", tag="x_raw", bufs=2)
            nc.sync.dma_start(out=x_raw[g][:, 0, :], in_=hf[g * P : (g + 1) * P, :])

        def load(j):
            if not 0 <= j < len(loads):
                return
            issued.append(j)
            layer, g, first_row, row_tiles, first_pass, n_passes = chunks[loads[j][0]]
            n_members = len(loads[j])
            raw[j] = raws.tile([P, C['load_mid'] * CHUNK_COLS], BF16, name="raw", tag="raw")
            if layer == 1:
                if first_row == 0 and not C['x_after']:
                    load_x(g)
                w_rows = g1_w[g, first_row : first_row + n_members * W1_ROWS, :]
                split = C['c0_split'] if j == 0 else 1
                per = n_members * 2 // split
                for s in range(split):
                    nc.sync.dma_start(
                        out=raw[j][:, s * per * 2 * H : (s + 1) * per * 2 * H].rearrange("p (u q) -> p u q", q=2 * H),
                        in_=w_rows[s * per * 256 : (s + 1) * per * 256, :].rearrange("(u p e) h -> p u (e h)", p=P, e=2),
                    )
                if first_row == 0 and C['x_after']:
                    load_x(g)
            else:
                w_rows = g2_w[g, first_row : first_row + n_members * row_tiles * P, first_pass * K_PASS : (first_pass + n_passes) * K_PASS]
                nc.sync.dma_start(
                    out=raw[j][:, 0 : n_members * row_tiles * n_passes * K_PASS].rearrange("p (c q) -> p c q", c=n_members * row_tiles),
                    in_=w_rows.rearrange("(c p r) i -> p (c r) i", c=n_members, p=P),
                )

        def flip(raw_rows, operand_tiles, grouped_tile, tailcopy=False):
            raw_words = raw_rows.bitcast(F32)
            grouped_words = grouped_tile[:].bitcast(F32)
            nb = (len(operand_tiles) + BANK_TILES - 1) // BANK_TILES
            for b in range(nb):
                tiles = operand_tiles[BANK_TILES * b : BANK_TILES * (b + 1)]
                bank = banks.tile([P, BANK_TILES, HALVES, P], F32, name="bank", tag="bank")
                for x, (row_tile, k_pass) in enumerate(tiles):
                    for u in range(HALVES):
                        first_word = WORDS_PASS * k_pass + P * u
                        nc.tensor.transpose(bank[:, x, u, :], raw_words[:, row_tile, first_word : first_word + P], ident[:])
                dst = grouped_words[:, BANK_TILES * b : BANK_TILES * b + len(tiles), :, :]
                src = bank[:, 0 : len(tiles), :, :].rearrange("p x u m -> p x m u")
                if tailcopy:
                    tail_emptied.append(b)
                    onv = len(tail_emptied) % C.get('tail_mod', 2) == 0
                else:
                    onv = len(emptied) % VECTOR_EVERY == VECTOR_EVERY - 1
                    emptied.append(b)
                if onv:
                    nc.vector.tensor_copy(out=dst, in_=src)
                else:
                    nc.scalar.copy(out=dst, in_=src)

        def spread_b2(g):
            b2_bank = banks.tile([P, H], BF16, name="b2_bank", tag="bank")
            for half in range(H // BANK):
                cols = slice(half * BANK, (half + 1) * BANK)
                nc.tensor.matmul(out=b2_bank[:, cols], lhsT=ident_bf[:, g : g + 1].to_broadcast([P, P]), rhs=b2_rows[:, cols], start=True, stop=True)
            (nc.vector.tensor_copy if C.get('xall') else nc.scalar.copy)(out=b2[g][:], in_=b2_bank[:])

        def flip_x(g):
            if C.get('xall'):
                return
            x_grouped[g] = work.tile([P, H_PASSES, P, PACK], BF16, name="x_grouped", align_bytes=64)
            flip(x_raw[g][:], [(0, a) for a in range(H_PASSES)], x_grouped[g])

        def flip_chunk(n):
            if not 0 <= n < n_chunks:
                return
            layer, g, first_row, row_tiles, first_pass, n_passes = chunks[n]
            first = layer == 1 and first_row == 0
            if first and not C['x_after']:
                flip_x(g)
                if C['spread'] == 'group':
                    spread_b2(g)
            grouped[n] = work.tile([P, CHUNK_TILES, P, PACK], BF16, name="grouped", align_bytes=64)
            if layer == 1:
                operand_tiles = [(t, a) for t in range(row_tiles) for a in range(H_PASSES)]
            else:
                operand_tiles = [(r, c) for c in range(n_passes) for r in range(row_tiles)]
            j, place = load_of[n]
            chunk_cols = slice(place * CHUNK_COLS, place * CHUNK_COLS + row_tiles * n_passes * K_PASS)
            flip(raw[j][:, chunk_cols].rearrange("p (t k) -> p t k", t=row_tiles), operand_tiles, grouped[n], tailcopy=(C['tailcopy'] and n >= n_chunks - C['tailcopy']))
            if first and C['x_after']:
                flip_x(g)
                if n == 0:
                    head_work()
                if C['spread'] == 'group':
                    spread_b2(g)
            if n == loads[j][-1]:
                load(j + RAW_BUFS)

        def quantise(n):
            if not 0 <= n < n_chunks:
                return
            layer, g, first_row, row_tiles, first_pass, n_passes = chunks[n]
            def quantise_x():
                if layer == 1 and first_row == 0 and not C.get('xall'):
                    nc.vector.quantize_mx(
                        out=x_codes[g][:].rearrange("p a k -> p (a k)").bitcast(FP8X4),
                        scales=x_scales[g][:].rearrange("p a k -> p (a k)"),
                        in_=x_grouped[g][:].rearrange("p a k t -> p (a k t)"),
                    )
            if not C['x_after']:
                quantise_x()
            tiles = row_tiles * n_passes
            codes[n] = work.tile([P, CHUNK_TILES * P], U32, name="codes", align_bytes=64)
            scales[n] = work.tile([P, CHUNK_TILES * P], U8, name="scales", align_bytes=64)
            nc.vector.quantize_mx(
                out=codes[n][:, 0 : tiles * P].bitcast(FP8X4),
                scales=scales[n][:, 0 : tiles * P],
                in_=grouped[n][:, 0:tiles, :, :].rearrange("p o m t -> p (o m t)"),
            )
            if C['x_after']:
                quantise_x()

        def multiply(n):
            if not 0 <= n < n_chunks:
                return
            layer, g, first_row, row_tiles, first_pass, n_passes = chunks[n]
            if layer == 1:
                y_bank = sums.tile([P, PACK, P], F32, name="y_bank", tag="sum")
                for t in range(row_tiles):
                    for a in range(H_PASSES):
                        cols = slice((H_PASSES * t + a) * P, (H_PASSES * t + a + 1) * P)
                        nc.tensor.matmul_mx(
                            out=y_bank[:, t, :], lhsT=codes[n][:, cols].bitcast(FP8X4), lhsT_scale=scales[n][:, cols],
                            rhs=(xa_codes[:, g, a, :] if C.get('xall') else x_codes[g][:, a, :]).bitcast(FP8X4), rhs_scale=(xa_scales[:, g, a, :] if C.get('xall') else x_scales[g][:, a, :]),
                            start=(a == 0), stop=(a == H_PASSES - 1),
                        )
                y_grouped[n] = work.tile([P, P, PACK], BF16, name="y_grouped", align_bytes=64)
                first_bias = PACK * (g * I + first_row) // K_PASS
                nc.vector.tensor_tensor(
                    out=y_grouped[n][:], in0=y_bank[:].rearrange("p t k -> p k t"),
                    in1=b1[:, first_bias : first_bias + PACK].unsqueeze(1).to_broadcast([P, P, PACK]), op=ADD,
                )
            else:
                width = row_tiles * P
                if first_pass == 0:
                    out_banks[(g, first_row)] = sums.tile([P, width], F32, name="out_bank", tag="sum")
                out_bank = out_banks[(g, first_row)]
                for c in range(n_passes):
                    cols = slice(c * width, (c + 1) * width)
                    cc = first_pass + c
                    nc.tensor.matmul_mx(
                        out=out_bank[:], lhsT=y_codes[g][:, cc, :].bitcast(FP8X4), lhsT_scale=y_scales[g][:, cc, :],
                        rhs=codes[n][:, cols].bitcast(FP8X4), rhs_scale=scales[n][:, cols],
                        start=(cc == 0), stop=(cc == I_PASSES - 1),
                    )
                if first_pass + n_passes < I_PASSES:
                    return
                if first_row == 0:
                    out_rows[g] = outs.tile([P, H], F32, name="out_rows")
                out_cols = slice(first_row, first_row + width)
                nc.vector.tensor_tensor(
                    out=out_rows[g][:, out_cols].rearrange("k (m r) -> k m r", r=row_tiles),
                    in0=out_bank[:].rearrange("k (r m) -> k m r", r=row_tiles),
                    in1=b2[g][:, out_cols].rearrange("k (m r) -> k m r", r=row_tiles), op=ADD,
                )

        def finish(n):
            if not 0 <= n < n_chunks:
                return
            layer, g, first_row, row_tiles, first_pass, n_passes = chunks[n]
            if layer == 1:
                c = first_row // K_PASS
                nc.vector.quantize_mx(out=y_codes[g][:, c, :].bitcast(FP8X4), scales=y_scales[g][:, c, :], in_=y_grouped[n][:].rearrange("p k t -> p (k t)"))
            elif first_pass + n_passes < I_PASSES:
                return
            elif g == GROUPS - 1:
                ready.append((g, first_row, row_tiles * P))
            elif first_row + row_tiles * P == H:
                ready.append((g, 0, H))

        b1_rows = keep.tile([P, 2 * P], BF16, name="b1_rows")
        nc.vector.memset(b1_rows[:].bitcast(I32), 0)
        b2_rows = keep.tile([P, H], BF16, name="b2_rows")
        nc.vector.memset(b2_rows[:].bitcast(I32), 0)
        n_b1_rows = GROUPS * I // (2 * P)
        def bias_loads(q):
            q.dma_start(out=b1_rows[0:n_b1_rows, :], in_=g1_b.rearrange("g (r q) -> (g r) q", q=2 * P))
            q.dma_start(out=b2_rows[0:GROUPS, :], in_=g2_b)
        if C['bias_q'] == 'sync_first':
            bias_loads(nc.sync)
        elif C['bias_q'] == 'scalar':
            bias_loads(nc.scalar)
        if C.get('xall'):
            nc.sync.dma_start(out=xa_raw[:], in_=hf.rearrange("(g p) h -> p g h", p=P))
        load(0)
        if C['bias_q'] == 'sync_second':
            bias_loads(nc.sync)
        for j in range(1, RAW_BUFS):
            load(j)

        b1 = keep.tile([P, 2 * n_b1_rows], BF16, name="b1")
        def head_work():
            b1_bank = banks.tile([P, P], F32, name="b1_bank", tag="bank")
            nc.tensor.transpose(b1_bank[:], b1_rows[:].bitcast(F32), ident[:])
            nc.vector.tensor_copy(out=b1[:].bitcast(F32), in_=b1_bank[:, 0:n_b1_rows])
            if C['spread'] == 'head':
                for g in range(GROUPS):
                    spread_b2(g)
        if not C['x_after']:
            head_work()
        if C.get('xall'):
            flip(xa_raw[:], [(g, a) for g in range(GROUPS) for a in range(H_PASSES)], xa_grouped)

        stored = 0
        R = lambda r: rounds[r] if 0 <= r < len(rounds) else []
        for r in range(len(rounds) + C['lagf']):
            if r == 1 and C.get('xall'):
                nc.vector.quantize_mx(out=xa_codes[:].rearrange("p g a k -> p (g a k)").bitcast(FP8X4), scales=xa_scales[:].rearrange("p g a k -> p (g a k)"), in_=xa_grouped[:].rearrange("p o k t -> p (o k t)"))
            qs, fs = R(r - C['lagq']), R(r - C['lagf'])
            for i in range(max(len(qs), len(fs))):
                if i < len(qs):
                    quantise(qs[i])
                if i < len(fs):
                    finish(fs[i])
            for n in R(r):
                flip_chunk(n)
            if len(issued) == len(loads):
                for g, first_col, width in ready[stored:]:
                    out_cols = slice(first_col, first_col + width)
                    nc.sync.dma_start(out=out[g * P : (g + 1) * P, out_cols], in_=out_rows[g][:, out_cols])
                stored = len(ready)
            for n in R(r - C['lagm']):
                multiply(n)
